import numpy as np
import ml_dtypes


def mxq(x, axis, fmt="e4m3"):
    dtype, down = {"e4m3": (ml_dtypes.float8_e4m3fn, 7), "e5m2": (ml_dtypes.float8_e5m2, 14)}[fmt]
    v = np.moveaxis(np.asarray(x, np.float32).astype(ml_dtypes.bfloat16).astype(np.float64), axis, -1)
    blocks = v.reshape(v.shape[:-1] + (-1, 32))
    amax = np.abs(blocks).max(-1, keepdims=True)
    byte = np.maximum(np.where(amax > 0, np.frexp(amax)[1] - 1 + 127, 0) - down, 1)
    scale = np.exp2(byte - 127.0)
    codes = (blocks / scale).astype(np.float32).astype(dtype).astype(np.float64)
    return np.moveaxis((codes * scale).reshape(v.shape), -1, axis)


WIDE = False


def mx_kscale(k):
    if not WIDE:
        return np.ones(k)
    levels = np.array([10, -10, 5, -5, 0])
    a = np.random.permutation(np.resize(levels, k // 512 * 4)).reshape(k // 512, 4)
    idx = np.arange(k)
    return np.exp2(a[idx // 512, idx % 128 // 32])


BF16 = ml_dtypes.bfloat16


def bf(x):
    return np.asarray(x, np.float32).astype(BF16)


def f64(x):
    return np.asarray(x).astype(np.float64)


E2M1 = np.array([0.0, 0.5, 1.0, 1.5, 2.0, 3.0, 4.0, 6.0, -0.0, -0.5, -1.0, -1.5, -2.0, -3.0, -4.0, -6.0])


def pack_weight(w, fmt):
    k, n = w.shape
    w = f64(bf(w)).reshape(k // 32, 32, n)
    amax = np.abs(w).max(1)
    if fmt == "e4m3":
        byte = np.frexp(amax)[1] - 1 + 127 - 7
    else:
        mant, ex = np.frexp(amax / 6.0)
        byte = np.where(mant > 0.5, ex, ex - 1) + 127
    byte = np.clip(np.where(amax > 0, byte, 1), 1, 254)
    scaled = (w * np.exp2(127.0 - byte)[:, None, :]).reshape(k, n).astype(np.float32)
    by_word = np.ascontiguousarray(scaled.reshape(k // 512, 128, 4, n).transpose(0, 1, 3, 2))
    if fmt == "e4m3":
        words = by_word.astype(ml_dtypes.float8_e4m3fn).view(np.uint8)
    else:
        c = by_word.astype(ml_dtypes.float4_e2m1fn).view(np.uint8) & 0xF
        words = c[..., 0::2] | (c[..., 1::2] << 4)
    return np.ascontiguousarray(words), np.ascontiguousarray(byte.astype(np.uint8).reshape(k // 512, 16, n))


def unpack_weight(words, scales, fmt):
    g, p, n, _ = words.shape
    if fmt == "e4m3":
        vals = np.ascontiguousarray(words).view(ml_dtypes.float8_e4m3fn).astype(np.float64)
    else:
        nib = np.empty((g, p, n, 4), np.uint8)
        nib[..., 0::2] = words & 0xF
        nib[..., 1::2] = words >> 4
        vals = E2M1[nib]
    vals = vals * np.repeat(np.exp2(scales.astype(np.float64) - 127.0), 8, axis=1)[..., None]
    return vals.transpose(0, 1, 3, 2).reshape(g * 512, n)


NB, C, O, CZ, DD, HH, WW, MG = 1, 512, 512, 512, 4, 8, 16, 4
STRIDES = (2, 2, 2)
FMT = "e4m3"


def setup_inputs():
    s = mx_kscale(C)
    sd, sh, sw = STRIDES
    x = bf(np.random.standard_normal((NB, C, DD, HH, WW)) * s[None, :, None, None, None])
    z = bf(np.random.standard_normal((NB, CZ, sd * DD + MG, sh * HH + MG, sw * WW + MG)))
    w_oc = np.random.standard_normal((O, C)) / np.sqrt(C) / s[None, :]
    words, scales = pack_weight(np.ascontiguousarray(w_oc.T), FMT)
    b = bf(np.random.standard_normal(O) * 0.5)
    return {"x": x, "z": z, "W_words": words, "W_scales": scales, "b": b}


def reference(x, z, W_words, W_scales, b):
    sd, sh, sw = STRIDES
    u = np.repeat(np.repeat(np.repeat(f64(x), sd, axis=2), sh, axis=3), sw, axis=4)
    n, c, d, h, w = u.shape
    y = unpack_weight(W_words, W_scales, FMT).T @ mxq(u.reshape(n, c, d * h * w), 1, "e4m3")
    y = y.reshape(n, -1, d, h, w) + f64(b)[None, :, None, None, None]
    zf = f64(z)
    off = [(zf.shape[i] - y.shape[i]) // 2 for i in range(2, 5)]
    zc = zf[:, :,
            off[0]:off[0] + y.shape[2],
            off[1]:off[1] + y.shape[3],
            off[2]:off[2] + y.shape[4]]
    return np.concatenate([y, zc], axis=1)

@@ -1,0 +1,149 @@
+from contextlib import ExitStack
+
+import concourse.mybir as mybir
+from concourse.masks import make_identity
+
+F32 = mybir.dt.float32
+BF16 = mybir.dt.bfloat16
+I32 = mybir.dt.int32
+U32 = mybir.dt.uint32
+U8 = mybir.dt.uint8
+FP8X4 = mybir.dt.float8_e4m3fn_x4
+
+P = 128
+PACK = 4
+C = P * PACK
+O = 512
+O_TILES = O // P
+CZ = 512
+Z_TILES = CZ // P
+
+XD, XH, XW = 4, 8, 16
+UP = 2
+UD, UH, UW = UP * XD, UP * XH, UP * XW
+POSITIONS = UD * UH * UW
+ZD, ZH, ZW = 12, 20, 36
+CROP = 2
+
+N_PASS = 512
+X_PLANES = N_PASS // (XH * UW)
+HALVES = XD // X_PLANES
+X_COLS = X_PLANES * XH * XW
+
+Z_FIRST = CROP * ZH * ZW + CROP * ZW
+Z_LAST = (CROP + UD - 1) * ZH * ZW + (CROP + UH) * ZW
+Z_RUN = Z_LAST - Z_FIRST
+
+PSUM_BANKS = 8
+
+FLOPS = 2 * C * O * POSITIONS
+BYTES = (
+    4 * (O + CZ) * POSITIONS
+    + 2 * CZ * POSITIONS
+    + 2 * C * XD * XH * XW
+    + C * O
+    + (C // 32) * O
+    + 2 * O
+)
+
+
+def tile_upconvcropcat_kernel(tc, x, z, W_words, W_scales, b, out):
+    nc = tc.nc
+
+    x_rows = x[0].rearrange("(p t) d h w -> p t (d h w)", t=PACK)
+    z_rows = z[0].rearrange("(p t) d h w -> p t (d h w)", t=Z_TILES)
+    y_out = out[0, 0:O].rearrange("(m p) d h w -> m p (d h w)", p=P)
+    zc_out = out[0, O : O + CZ].rearrange("(p t) d h w -> p t (d h w)", t=Z_TILES)
+
+    with ExitStack() as ctx:
+        keep = ctx.enter_context(tc.tile_pool(name="keep", bufs=1))
+        z_pool = ctx.enter_context(tc.tile_pool(name="z_pool", bufs=Z_TILES))
+        zc_pool = ctx.enter_context(tc.tile_pool(name="zc_pool", bufs=Z_TILES))
+        y_pool = ctx.enter_context(tc.tile_pool(name="y_pool", bufs=O_TILES))
+        bias_psum = ctx.enter_context(tc.psum_pool(name="bias_psum", bufs=1))
+        acc_psum = ctx.enter_context(tc.psum_pool(name="acc_psum", bufs=PSUM_BANKS - 1))
+
+        w_scales = keep.tile([P, O], U8, align_bytes=64)
+        nc.vector.memset(w_scales[:].bitcast(I32), 0)
+        b_rows = keep.tile([P, P], BF16)
+        nc.vector.memset(b_rows[:], 0.0)
+        identity = keep.tile([P, P], BF16)
+        make_identity(nc, identity[:])
+
+        x_raw = keep.tile([P, PACK, XD * XH * XW], BF16)
+        nc.sync.dma_start(out=x_raw[:], in_=x_rows)
+        w_words = keep.tile([P, O], U32, align_bytes=64)
+        nc.sync.dma_start(
+            out=w_words[:].bitcast(I32),
+            in_=W_words[0].rearrange("p n t -> p (n t)").bitcast(I32),
+        )
+        for quadrant in range(4):
+            nc.sync.dma_start(
+                out=w_scales[32 * quadrant : 32 * quadrant + 4, :].bitcast(I32),
+                in_=W_scales[0, 4 * quadrant : 4 * quadrant + 4, :].bitcast(I32),
+            )
+        nc.sync.dma_start(out=b_rows[0:O_TILES, :], in_=b.rearrange("(m p) -> m p", p=P))
+        z_raw = []
+        for t in range(Z_TILES):
+            z_tile = z_pool.tile([P, UD, ZH, ZW], BF16, name="z_tile")
+            nc.sync.dma_start(
+                out=z_tile[:].rearrange("p d h w -> p (d h w)")[:, 0:Z_RUN],
+                in_=z_rows[:, t, Z_FIRST:Z_LAST],
+            )
+            z_raw.append(z_tile)
+
+        u_grouped = keep.tile([P, HALVES, X_COLS, UP, PACK], BF16, align_bytes=64)
+        u_codes = keep.tile([P, HALVES, N_PASS], U32, align_bytes=64)
+        u_scales = keep.tile([P, HALVES, N_PASS], U8, align_bytes=64)
+        for half in range(HALVES):
+            nc.vector.tensor_copy(
+                out=u_grouped[:, half],
+                in_=x_raw[:, :, half * X_COLS : (half + 1) * X_COLS]
+                .rearrange("p t q -> p q t")
+                .unsqueeze(2)
+                .to_broadcast([P, X_COLS, UP, PACK]),
+            )
+        for half in range(HALVES):
+            nc.vector.quantize_mx(
+                out=u_codes[:, half].bitcast(FP8X4),
+                scales=u_scales[:, half],
+                in_=u_grouped[:, half].rearrange("p q k t -> p (q k t)"),
+            )
+
+        b_columns = bias_psum.tile([P, P], BF16)
+        nc.tensor.transpose(b_columns[:], b_rows[:], identity[:])
+        bias = keep.tile([P, O_TILES], F32)
+        nc.vector.tensor_copy(out=bias[:], in_=b_columns[:, 0:O_TILES])
+
+        for m in range(O_TILES):
+            m_cols = slice(m * P, (m + 1) * P)
+            y_sb = y_pool.tile([P, HALVES, X_PLANES, UP, XH, UP, UW], F32, name="y_sb")
+            for half in range(HALVES):
+                for depth_copy in range(UP):
+                    for height_copy in range(UP):
+                        acc = acc_psum.tile([P, N_PASS], F32, name="acc")
+                        nc.tensor.matmul_mx(
+                            out=acc[:],
+                            lhsT=w_words[:, m_cols].bitcast(FP8X4),
+                            lhsT_scale=w_scales[:, m_cols],
+                            rhs=u_codes[:, half].bitcast(FP8X4),
+                            rhs_scale=u_scales[:, half],
+                            start=True,
+                            stop=True,
+                        )
+                        nc.scalar.activation(
+                            out=y_sb[:, half, :, depth_copy, :, height_copy, :],
+                            in_=acc[:].rearrange("p (e h w) -> p e h w", e=X_PLANES, h=XH),
+                            func=mybir.ActivationFunctionType.Identity,
+                            bias=bias[:, m : m + 1],
+                        )
+            nc.scalar.dma_start(
+                out=y_out[m], in_=y_sb[:].rearrange("p s e a h c w -> p (s e a h c w)")
+            )
+
+        for t in range(Z_TILES):
+            zc_sb = zc_pool.tile([P, UD, UH, UW], F32, name="zc_sb")
+            nc.vector.tensor_copy(out=zc_sb[:], in_=z_raw[t][:, :, 0:UH, CROP : CROP + UW])
+            nc.sync.dma_start(
+                out=zc_out[:, t], in_=zc_sb[:].rearrange("p d h w -> p (d h w)")
+            )

@@ -17,6 +17,8 @@ O = 512
 O_TILES = O // P
 CZ = 512
 Z_TILES = CZ // P
+assert O_TILES == Z_TILES
+OUT_TILES = O_TILES
 
 XD, XH, XW = 4, 8, 16
 UP = 2
@@ -115,8 +117,14 @@ def tile_upconvcropcat_kernel(tc, x, z, W_words, W_scales, b, out):
         bias = keep.tile([P, O_TILES], F32)
         nc.vector.tensor_copy(out=bias[:], in_=b_columns[:, 0:O_TILES])
 
-        for m in range(O_TILES):
-            m_cols = slice(m * P, (m + 1) * P)
+        for i in range(OUT_TILES):
+            zc_sb = zc_pool.tile([P, UD, UH, UW], F32, name="zc_sb")
+            nc.vector.tensor_copy(out=zc_sb[:], in_=z_raw[i][:, :, 0:UH, CROP : CROP + UW])
+            nc.sync.dma_start(
+                out=zc_out[:, i], in_=zc_sb[:].rearrange("p d h w -> p (d h w)")
+            )
+
+            o_cols = slice(i * P, (i + 1) * P)
             y_sb = y_pool.tile([P, HALVES, X_PLANES, UP, XH, UP, UW], F32, name="y_sb")
             for half in range(HALVES):
                 for depth_copy in range(UP):
@@ -124,8 +132,8 @@ def tile_upconvcropcat_kernel(tc, x, z, W_words, W_scales, b, out):
                         acc = acc_psum.tile([P, N_PASS], F32, name="acc")
                         nc.tensor.matmul_mx(
                             out=acc[:],
-                            lhsT=w_words[:, m_cols].bitcast(FP8X4),
-                            lhsT_scale=w_scales[:, m_cols],
+                            lhsT=w_words[:, o_cols].bitcast(FP8X4),
+                            lhsT_scale=w_scales[:, o_cols],
                             rhs=u_codes[:, half].bitcast(FP8X4),
                             rhs_scale=u_scales[:, half],
                             start=True,
@@ -135,15 +143,8 @@ def tile_upconvcropcat_kernel(tc, x, z, W_words, W_scales, b, out):
                             out=y_sb[:, half, :, depth_copy, :, height_copy, :],
                             in_=acc[:].rearrange("p (e h w) -> p e h w", e=X_PLANES, h=XH),
                             func=mybir.ActivationFunctionType.Identity,
-                            bias=bias[:, m : m + 1],
+                            bias=bias[:, i : i + 1],
                         )
-            nc.scalar.dma_start(
-                out=y_out[m], in_=y_sb[:].rearrange("p s e a h c w -> p (s e a h c w)")
-            )
-
-        for t in range(Z_TILES):
-            zc_sb = zc_pool.tile([P, UD, UH, UW], F32, name="zc_sb")
-            nc.vector.tensor_copy(out=zc_sb[:], in_=z_raw[t][:, :, 0:UH, CROP : CROP + UW])
             nc.sync.dma_start(
-                out=zc_out[:, t], in_=zc_sb[:].rearrange("p d h w -> p (d h w)")
+                out=y_out[i], in_=y_sb[:].rearrange("p s e a h c w -> p (s e a h c w)")
             )

@@ -1,7 +1,6 @@
 from contextlib import ExitStack
 
 import concourse.mybir as mybir
-from concourse.masks import make_identity
 
 F32 = mybir.dt.float32
 BF16 = mybir.dt.bfloat16
@@ -14,11 +13,9 @@ P = 128
 PACK = 4
 C = P * PACK
 O = 512
-O_TILES = O // P
 CZ = 512
-Z_TILES = CZ // P
-assert O_TILES == Z_TILES
-OUT_TILES = O_TILES
+GROUP = 4
+assert O == GROUP * P and CZ == GROUP * P
 
 XD, XH, XW = 4, 8, 16
 UP = 2
@@ -37,6 +34,8 @@ Z_LAST = (CROP + UD - 1) * ZH * ZW + (CROP + UH) * ZW
 Z_RUN = Z_LAST - Z_FIRST
 
 PSUM_BANKS = 8
+ZC_STORES = 2
+ZC_WIDTH = GROUP // ZC_STORES
 
 FLOPS = 2 * C * O * POSITIONS
 BYTES = (
@@ -53,40 +52,35 @@ def tile_upconvcropcat_kernel(tc, x, z, W_words, W_scales, b, out):
     nc = tc.nc
 
     x_rows = x[0].rearrange("(p t) d h w -> p t (d h w)", t=PACK)
-    z_rows = z[0].rearrange("(p t) d h w -> p t (d h w)", t=Z_TILES)
-    y_out = out[0, 0:O].rearrange("(m p) d h w -> m p (d h w)", p=P)
-    zc_out = out[0, O : O + CZ].rearrange("(p t) d h w -> p t (d h w)", t=Z_TILES)
+    z_rows = z[0].rearrange("(p t) d h w -> p t (d h w)", t=GROUP)
+    y_out = out[0, 0:O].rearrange("(p m) d h w -> p m (d h w)", m=GROUP)
+    zc_out = out[0, O : O + CZ].rearrange("(p t) d h w -> p t (d h w)", t=GROUP)
 
     with ExitStack() as ctx:
         keep = ctx.enter_context(tc.tile_pool(name="keep", bufs=1))
-        z_pool = ctx.enter_context(tc.tile_pool(name="z_pool", bufs=Z_TILES))
-        zc_pool = ctx.enter_context(tc.tile_pool(name="zc_pool", bufs=Z_TILES))
-        y_pool = ctx.enter_context(tc.tile_pool(name="y_pool", bufs=O_TILES))
-        bias_psum = ctx.enter_context(tc.psum_pool(name="bias_psum", bufs=1))
-        acc_psum = ctx.enter_context(tc.psum_pool(name="acc_psum", bufs=PSUM_BANKS - 1))
+        z_pool = ctx.enter_context(tc.tile_pool(name="z_pool", bufs=GROUP))
+        zc_pool = ctx.enter_context(tc.tile_pool(name="zc_pool", bufs=ZC_STORES))
+        acc_psum = ctx.enter_context(tc.psum_pool(name="acc_psum", bufs=PSUM_BANKS))
 
-        w_scales = keep.tile([P, O], U8, align_bytes=64)
-        nc.vector.memset(w_scales[:].bitcast(I32), 0)
-        b_rows = keep.tile([P, P], BF16)
-        nc.vector.memset(b_rows[:], 0.0)
-        identity = keep.tile([P, P], BF16)
-        make_identity(nc, identity[:])
+        s_raw = keep.tile([P, O], U8, align_bytes=64)
+        nc.vector.memset(s_raw[:].bitcast(I32), 0)
 
         x_raw = keep.tile([P, PACK, XD * XH * XW], BF16)
         nc.sync.dma_start(out=x_raw[:], in_=x_rows)
-        w_words = keep.tile([P, O], U32, align_bytes=64)
+        w_raw = keep.tile([P, O], U32, align_bytes=64)
         nc.sync.dma_start(
-            out=w_words[:].bitcast(I32),
+            out=w_raw[:].bitcast(I32),
             in_=W_words[0].rearrange("p n t -> p (n t)").bitcast(I32),
         )
         for quadrant in range(4):
             nc.sync.dma_start(
-                out=w_scales[32 * quadrant : 32 * quadrant + 4, :].bitcast(I32),
+                out=s_raw[32 * quadrant : 32 * quadrant + 4, :].bitcast(I32),
                 in_=W_scales[0, 4 * quadrant : 4 * quadrant + 4, :].bitcast(I32),
             )
-        nc.sync.dma_start(out=b_rows[0:O_TILES, :], in_=b.rearrange("(m p) -> m p", p=P))
+        b_raw = keep.tile([P, GROUP], BF16)
+        nc.sync.dma_start(out=b_raw[:], in_=b.rearrange("(p m) -> p m", m=GROUP))
         z_raw = []
-        for t in range(Z_TILES):
+        for t in range(GROUP):
             z_tile = z_pool.tile([P, UD, ZH, ZW], BF16, name="z_tile")
             nc.sync.dma_start(
                 out=z_tile[:].rearrange("p d h w -> p (d h w)")[:, 0:Z_RUN],
@@ -105,6 +99,21 @@ def tile_upconvcropcat_kernel(tc, x, z, W_words, W_scales, b, out):
                 .unsqueeze(2)
                 .to_broadcast([P, X_COLS, UP, PACK]),
             )
+
+        w_words = keep.tile([P, GROUP, P], U32, align_bytes=64)
+        nc.vector.tensor_copy(
+            out=w_words[:].bitcast(I32),
+            in_=w_raw[:].bitcast(I32).rearrange("p (j m) -> p m j", m=GROUP),
+        )
+        w_scales = keep.tile([P, GROUP, P], U8, align_bytes=64)
+        for m in range(GROUP):
+            nc.vector.tensor_copy(
+                out=w_scales[:, m, :],
+                in_=s_raw[:].rearrange("p (j m) -> p m j", m=GROUP)[:, m, :],
+            )
+        bias = keep.tile([P, GROUP], F32)
+        nc.vector.tensor_copy(out=bias[:], in_=b_raw[:])
+
         for half in range(HALVES):
             nc.vector.quantize_mx(
                 out=u_codes[:, half].bitcast(FP8X4),
@@ -112,39 +121,53 @@ def tile_upconvcropcat_kernel(tc, x, z, W_words, W_scales, b, out):
                 in_=u_grouped[:, half].rearrange("p q k t -> p (q k t)"),
             )
 
-        b_columns = bias_psum.tile([P, P], BF16)
-        nc.tensor.transpose(b_columns[:], b_rows[:], identity[:])
-        bias = keep.tile([P, O_TILES], F32)
-        nc.vector.tensor_copy(out=bias[:], in_=b_columns[:, 0:O_TILES])
+        zc_sb = []
 
-        for i in range(OUT_TILES):
-            zc_sb = zc_pool.tile([P, UD, UH, UW], F32, name="zc_sb")
-            nc.vector.tensor_copy(out=zc_sb[:], in_=z_raw[i][:, :, 0:UH, CROP : CROP + UW])
-            nc.sync.dma_start(
-                out=zc_out[:, i], in_=zc_sb[:].rearrange("p d h w -> p (d h w)")
+        def widen(t):
+            if t % ZC_WIDTH == 0:
+                zc_sb.append(zc_pool.tile([P, ZC_WIDTH, UD, UH, UW], F32, name="zc_part"))
+            nc.vector.tensor_copy(
+                out=zc_sb[t // ZC_WIDTH][:, t % ZC_WIDTH],
+                in_=z_raw[t][:, :, 0:UH, CROP : CROP + UW],
             )
 
-            o_cols = slice(i * P, (i + 1) * P)
-            y_sb = y_pool.tile([P, HALVES, X_PLANES, UP, XH, UP, UW], F32, name="y_sb")
+        def store_zc(s):
+            nc.sync.dma_start(
+                out=zc_out[:, s * ZC_WIDTH : (s + 1) * ZC_WIDTH],
+                in_=zc_sb[s][:].rearrange("p t d h w -> p t (d h w)"),
+            )
+
+        widen(0)
+        widen(1)
+        store_zc(0)
+
+        widen(2)
+        widen(3)
+        store_zc(1)
+
+        y_sb = keep.tile([P, GROUP, HALVES, X_PLANES, UP, XH, UP, UW], F32)
+        for m in range(GROUP):
             for half in range(HALVES):
                 for depth_copy in range(UP):
                     for height_copy in range(UP):
                         acc = acc_psum.tile([P, N_PASS], F32, name="acc")
                         nc.tensor.matmul_mx(
                             out=acc[:],
-                            lhsT=w_words[:, o_cols].bitcast(FP8X4),
-                            lhsT_scale=w_scales[:, o_cols],
+                            lhsT=w_words[:, m, :].bitcast(FP8X4),
+                            lhsT_scale=w_scales[:, m, :],
                             rhs=u_codes[:, half].bitcast(FP8X4),
                             rhs_scale=u_scales[:, half],
                             start=True,
                             stop=True,
                         )
+                        dst = y_sb[:, m, half, :, depth_copy, :, height_copy, :]
+                        src = acc[:].rearrange("p (e h w) -> p e h w", e=X_PLANES, h=XH)
                         nc.scalar.activation(
-                            out=y_sb[:, half, :, depth_copy, :, height_copy, :],
-                            in_=acc[:].rearrange("p (e h w) -> p e h w", e=X_PLANES, h=XH),
+                            out=dst,
+                            in_=src,
                             func=mybir.ActivationFunctionType.Identity,
-                            bias=bias[:, i : i + 1],
+                            bias=bias[:, m : m + 1],
                         )
-            nc.sync.dma_start(
-                out=y_out[i], in_=y_sb[:].rearrange("p s e a h c w -> p (s e a h c w)")
-            )
+        nc.sync.dma_start(
+            out=y_out, in_=y_sb[:].rearrange("p m s e a h c w -> p m (s e a h c w)")
+        )

@@ -72,10 +72,10 @@ def tile_upconvcropcat_kernel(tc, x, z, W_words, W_scales, b, out):
             out=w_raw[:].bitcast(I32),
             in_=W_words[0].rearrange("p n t -> p (n t)").bitcast(I32),
         )
-        for quadrant in range(4):
+        for r in range(4):
             nc.sync.dma_start(
-                out=s_raw[32 * quadrant : 32 * quadrant + 4, :].bitcast(I32),
-                in_=W_scales[0, 4 * quadrant : 4 * quadrant + 4, :].bitcast(I32),
+                out=s_raw[r:P:32, :].bitcast(I32),
+                in_=W_scales[0, r:16:4, :].bitcast(I32),
             )
         b_raw = keep.tile([P, GROUP], BF16)
         nc.sync.dma_start(out=b_raw[:], in_=b.rearrange("(p m) -> p m", m=GROUP))

@@ -72,6 +72,17 @@ def tile_upconvcropcat_kernel(tc, x, z, W_words, W_scales, b, out):
             out=w_raw[:].bitcast(I32),
             in_=W_words[0].rearrange("p n t -> p (n t)").bitcast(I32),
         )
+        z_raw = []
+
+        def load_z(t):
+            z_tile = z_pool.tile([P, UD, ZH, ZW], BF16, name="z_tile")
+            nc.sync.dma_start(
+                out=z_tile[:].rearrange("p d h w -> p (d h w)")[:, 0:Z_RUN],
+                in_=z_rows[:, t, Z_FIRST:Z_LAST],
+            )
+            z_raw.append(z_tile)
+
+        load_z(0)
         for r in range(4):
             nc.sync.dma_start(
                 out=s_raw[r:P:32, :].bitcast(I32),
@@ -79,14 +90,8 @@ def tile_upconvcropcat_kernel(tc, x, z, W_words, W_scales, b, out):
             )
         b_raw = keep.tile([P, GROUP], BF16)
         nc.sync.dma_start(out=b_raw[:], in_=b.rearrange("(p m) -> p m", m=GROUP))
-        z_raw = []
-        for t in range(GROUP):
-            z_tile = z_pool.tile([P, UD, ZH, ZW], BF16, name="z_tile")
-            nc.sync.dma_start(
-                out=z_tile[:].rearrange("p d h w -> p (d h w)")[:, 0:Z_RUN],
-                in_=z_rows[:, t, Z_FIRST:Z_LAST],
-            )
-            z_raw.append(z_tile)
+        for t in range(1, GROUP):
+            load_z(t)
 
         u_grouped = keep.tile([P, HALVES, X_COLS, UP, PACK], BF16, align_bytes=64)
         u_codes = keep.tile([P, HALVES, N_PASS], U32, align_bytes=64)

@@ -33,7 +33,7 @@ Z_FIRST = CROP * ZH * ZW + CROP * ZW
 Z_LAST = (CROP + UD - 1) * ZH * ZW + (CROP + UH) * ZW
 Z_RUN = Z_LAST - Z_FIRST
 
-PSUM_BANKS = 8
+PSUM_BANKS = 7
 ZC_STORES = 2
 ZC_WIDTH = GROUP // ZC_STORES
 
@@ -61,9 +61,14 @@ def tile_upconvcropcat_kernel(tc, x, z, W_words, W_scales, b, out):
         z_pool = ctx.enter_context(tc.tile_pool(name="z_pool", bufs=GROUP))
         zc_pool = ctx.enter_context(tc.tile_pool(name="zc_pool", bufs=ZC_STORES))
         acc_psum = ctx.enter_context(tc.psum_pool(name="acc_psum", bufs=PSUM_BANKS))
+        bias_psum = ctx.enter_context(tc.psum_pool(name="bias_psum", bufs=1))
 
         s_raw = keep.tile([P, O], U8, align_bytes=64)
         nc.vector.memset(s_raw[:].bitcast(I32), 0)
+        b_row = keep.tile([P, O], BF16)
+        nc.vector.memset(b_row[:], 0.0)
+        ones = keep.tile([P, 1], BF16)
+        nc.vector.memset(ones[:], 1.0)
 
         x_raw = keep.tile([P, PACK, XD * XH * XW], BF16)
         nc.sync.dma_start(out=x_raw[:], in_=x_rows)
@@ -88,8 +93,7 @@ def tile_upconvcropcat_kernel(tc, x, z, W_words, W_scales, b, out):
                 out=s_raw[r:P:32, :].bitcast(I32),
                 in_=W_scales[0, r:16:4, :].bitcast(I32),
             )
-        b_raw = keep.tile([P, GROUP], BF16)
-        nc.sync.dma_start(out=b_raw[:], in_=b.rearrange("(p m) -> p m", m=GROUP))
+        nc.sync.dma_start(out=b_row[0:1, :], in_=b.rearrange("(r n) -> r n", r=1))
         for t in range(1, GROUP):
             load_z(t)
 
@@ -117,7 +121,16 @@ def tile_upconvcropcat_kernel(tc, x, z, W_words, W_scales, b, out):
                 in_=s_raw[:].rearrange("p (j m) -> p m j", m=GROUP)[:, m, :],
             )
         bias = keep.tile([P, GROUP], F32)
-        nc.vector.tensor_copy(out=bias[:], in_=b_raw[:])
+        bias_acc = bias_psum.tile([P, GROUP], F32)
+        for m in range(GROUP):
+            nc.tensor.matmul(
+                out=bias_acc[:, m : m + 1],
+                lhsT=b_row[:].rearrange("p (j m) -> p m j", m=GROUP)[:, m, :],
+                rhs=ones[:],
+                start=True,
+                stop=True,
+            )
+        nc.vector.tensor_copy(out=bias[:], in_=bias_acc[:])
 
         for half in range(HALVES):
             nc.vector.quantize_mx(

@@ -70,9 +70,9 @@ def tile_upconvcropcat_kernel(tc, x, z, W_words, W_scales, b, out):
         ones = keep.tile([P, 1], BF16)
         nc.vector.memset(ones[:], 1.0)
 
-        x_raw = keep.tile([P, PACK, XD * XH * XW], BF16)
+        x_raw = keep.tile([P, PACK, XD * XH * XW], BF16, align_bytes=512)
         nc.sync.dma_start(out=x_raw[:], in_=x_rows)
-        w_raw = keep.tile([P, O], U32, align_bytes=64)
+        w_raw = keep.tile([P, O], U32, align_bytes=512)
         nc.sync.dma_start(
             out=w_raw[:].bitcast(I32),
             in_=W_words[0].rearrange("p n t -> p (n t)").bitcast(I32),
@@ -80,7 +80,7 @@ def tile_upconvcropcat_kernel(tc, x, z, W_words, W_scales, b, out):
         z_raw = []
 
         def load_z(t):
-            z_tile = z_pool.tile([P, UD, ZH, ZW], BF16, name="z_tile")
+            z_tile = z_pool.tile([P, UD, ZH, ZW], BF16, name="z_tile", align_bytes=512)
             nc.sync.dma_start(
                 out=z_tile[:].rearrange("p d h w -> p (d h w)")[:, 0:Z_RUN],
                 in_=z_rows[:, t, Z_FIRST:Z_LAST],
@@ -143,7 +143,11 @@ def tile_upconvcropcat_kernel(tc, x, z, W_words, W_scales, b, out):
 
         def widen(t):
             if t % ZC_WIDTH == 0:
-                zc_sb.append(zc_pool.tile([P, ZC_WIDTH, UD, UH, UW], F32, name="zc_part"))
+                zc_sb.append(
+                    zc_pool.tile(
+                        [P, ZC_WIDTH, UD, UH, UW], F32, name="zc_part", align_bytes=512
+                    )
+                )
             nc.vector.tensor_copy(
                 out=zc_sb[t // ZC_WIDTH][:, t % ZC_WIDTH],
                 in_=z_raw[t][:, :, 0:UH, CROP : CROP + UW],
@@ -163,7 +167,7 @@ def tile_upconvcropcat_kernel(tc, x, z, W_words, W_scales, b, out):
         widen(3)
         store_zc(1)
 
-        y_sb = keep.tile([P, GROUP, HALVES, X_PLANES, UP, XH, UP, UW], F32)
+        y_sb = keep.tile([P, GROUP, HALVES, X_PLANES, UP, XH, UP, UW], F32, align_bytes=512)
         for m in range(GROUP):
             for half in range(HALVES):
                 for depth_copy in range(UP):

from contextlib import ExitStack

import concourse.mybir as mybir

F32 = mybir.dt.float32
BF16 = mybir.dt.bfloat16
I32 = mybir.dt.int32
U32 = mybir.dt.uint32
U8 = mybir.dt.uint8
FP8X4 = mybir.dt.float8_e4m3fn_x4

P = 128
PACK = 4
C = P * PACK
O = 512
CZ = 512
GROUP = 4
assert O == GROUP * P and CZ == GROUP * P

XD, XH, XW = 4, 8, 16
UP = 2
UD, UH, UW = UP * XD, UP * XH, UP * XW
POSITIONS = UD * UH * UW
ZD, ZH, ZW = 12, 20, 36
CROP = 2

N_PASS = 512
X_PLANES = N_PASS // (XH * UW)
HALVES = XD // X_PLANES
X_COLS = X_PLANES * XH * XW

Z_FIRST = CROP * ZH * ZW + CROP * ZW
Z_LAST = (CROP + UD - 1) * ZH * ZW + (CROP + UH) * ZW
Z_RUN = Z_LAST - Z_FIRST

PSUM_BANKS = 7
ZC_STORES = 2
ZC_WIDTH = GROUP // ZC_STORES

FLOPS = 2 * C * O * POSITIONS
BYTES = (
    4 * (O + CZ) * POSITIONS
    + 2 * CZ * POSITIONS
    + 2 * C * XD * XH * XW
    + C * O
    + (C // 32) * O
    + 2 * O
)


def tile_upconvcropcat_kernel(tc, x, z, W_words, W_scales, b, out):
    nc = tc.nc

    x_rows = x[0].rearrange("(p t) d h w -> p t (d h w)", t=PACK)
    z_rows = z[0].rearrange("(p t) d h w -> p t (d h w)", t=GROUP)
    y_out = out[0, 0:O].rearrange("(p m) d h w -> p m (d h w)", m=GROUP)
    zc_out = out[0, O : O + CZ].rearrange("(p t) d h w -> p t (d h w)", t=GROUP)

    with ExitStack() as ctx:
        keep = ctx.enter_context(tc.tile_pool(name="keep", bufs=1))
        z_pool = ctx.enter_context(tc.tile_pool(name="z_pool", bufs=GROUP))
        zc_pool = ctx.enter_context(tc.tile_pool(name="zc_pool", bufs=ZC_STORES))
        acc_psum = ctx.enter_context(tc.psum_pool(name="acc_psum", bufs=PSUM_BANKS))
        bias_psum = ctx.enter_context(tc.psum_pool(name="bias_psum", bufs=1))

        s_raw = keep.tile([P, O], U8, align_bytes=64)
        nc.vector.memset(s_raw[:].bitcast(I32), 0)
        b_row = keep.tile([P, O], BF16)
        nc.vector.memset(b_row[:], 0.0)
        ones = keep.tile([P, 1], BF16)
        nc.vector.memset(ones[:], 1.0)

        x_raw = keep.tile([P, PACK, XD * XH * XW], BF16, align_bytes=512)
        nc.sync.dma_start(out=x_raw[:], in_=x_rows)
        w_raw = keep.tile([P, O], U32, align_bytes=512)
        nc.sync.dma_start(
            out=w_raw[:].bitcast(I32),
            in_=W_words[0].rearrange("p n t -> p (n t)").bitcast(I32),
        )
        z_raw = []

        def load_z(t):
            z_tile = z_pool.tile([P, UD, ZH, ZW], BF16, name="z_tile", align_bytes=512)
            nc.sync.dma_start(
                out=z_tile[:].rearrange("p d h w -> p (d h w)")[:, 0:Z_RUN],
                in_=z_rows[:, t, Z_FIRST:Z_LAST],
            )
            z_raw.append(z_tile)

        load_z(0)
        for r in range(4):
            nc.sync.dma_start(
                out=s_raw[r:P:32, :].bitcast(I32),
                in_=W_scales[0, r:16:4, :].bitcast(I32),
            )
        nc.sync.dma_start(out=b_row[0:1, :], in_=b.rearrange("(r n) -> r n", r=1))
        for t in range(1, GROUP):
            load_z(t)

        u_grouped = keep.tile([P, HALVES, X_COLS, UP, PACK], BF16, align_bytes=64)
        u_codes = keep.tile([P, HALVES, N_PASS], U32, align_bytes=64)
        u_scales = keep.tile([P, HALVES, N_PASS], U8, align_bytes=64)
        for half in range(HALVES):
            nc.vector.tensor_copy(
                out=u_grouped[:, half],
                in_=x_raw[:, :, half * X_COLS : (half + 1) * X_COLS]
                .rearrange("p t q -> p q t")
                .unsqueeze(2)
                .to_broadcast([P, X_COLS, UP, PACK]),
            )

        w_words = keep.tile([P, GROUP, P], U32, align_bytes=64)
        nc.vector.tensor_copy(
            out=w_words[:].bitcast(I32),
            in_=w_raw[:].bitcast(I32).rearrange("p (j m) -> p m j", m=GROUP),
        )
        w_scales = keep.tile([P, GROUP, P], U8, align_bytes=64)
        for m in range(GROUP):
            nc.vector.tensor_copy(
                out=w_scales[:, m, :],
                in_=s_raw[:].rearrange("p (j m) -> p m j", m=GROUP)[:, m, :],
            )
        bias = keep.tile([P, GROUP], F32)
        bias_acc = bias_psum.tile([P, GROUP], F32)
        for m in range(GROUP):
            nc.tensor.matmul(
                out=bias_acc[:, m : m + 1],
                lhsT=b_row[:].rearrange("p (j m) -> p m j", m=GROUP)[:, m, :],
                rhs=ones[:],
                start=True,
                stop=True,
            )
        nc.vector.tensor_copy(out=bias[:], in_=bias_acc[:])

        for half in range(HALVES):
            nc.vector.quantize_mx(
                out=u_codes[:, half].bitcast(FP8X4),
                scales=u_scales[:, half],
                in_=u_grouped[:, half].rearrange("p q k t -> p (q k t)"),
            )

        zc_sb = []

        def widen(t):
            if t % ZC_WIDTH == 0:
                zc_sb.append(
                    zc_pool.tile(
                        [P, ZC_WIDTH, UD, UH, UW], F32, name="zc_part", align_bytes=512
                    )
                )
            nc.vector.tensor_copy(
                out=zc_sb[t // ZC_WIDTH][:, t % ZC_WIDTH],
                in_=z_raw[t][:, :, 0:UH, CROP : CROP + UW],
            )

        def store_zc(s):
            nc.sync.dma_start(
                out=zc_out[:, s * ZC_WIDTH : (s + 1) * ZC_WIDTH],
                in_=zc_sb[s][:].rearrange("p t d h w -> p t (d h w)"),
            )

        widen(0)
        widen(1)
        store_zc(0)

        widen(2)
        widen(3)
        store_zc(1)

        y_sb = keep.tile([P, GROUP, HALVES, X_PLANES, UP, XH, UP, UW], F32, align_bytes=512)
        for m in range(GROUP):
            for half in range(HALVES):
                for depth_copy in range(UP):
                    for height_copy in range(UP):
                        acc = acc_psum.tile([P, N_PASS], F32, name="acc")
                        nc.tensor.matmul_mx(
                            out=acc[:],
                            lhsT=w_words[:, m, :].bitcast(FP8X4),
                            lhsT_scale=w_scales[:, m, :],
                            rhs=u_codes[:, half].bitcast(FP8X4),
                            rhs_scale=u_scales[:, half],
                            start=True,
                            stop=True,
                        )
                        dst = y_sb[:, m, half, :, depth_copy, :, height_copy, :]
                        src = acc[:].rearrange("p (e h w) -> p e h w", e=X_PLANES, h=XH)
                        nc.scalar.activation(
                            out=dst,
                            in_=src,
                            func=mybir.ActivationFunctionType.Identity,
                            bias=bias[:, m : m + 1],
                        )
        nc.sync.dma_start(
            out=y_out, in_=y_sb[:].rearrange("p m s e a h c w -> p m (s e a h c w)")
        )
